import numpy as np
import ml_dtypes


def mxq(x, axis, fmt="e4m3"):
    dtype, down = {"e4m3": (ml_dtypes.float8_e4m3fn, 7), "e5m2": (ml_dtypes.float8_e5m2, 14)}[fmt]
    v = np.moveaxis(np.asarray(x, np.float32).astype(ml_dtypes.bfloat16).astype(np.float64), axis, -1)
    blocks = v.reshape(v.shape[:-1] + (-1, 32))
    amax = np.abs(blocks).max(-1, keepdims=True)
    byte = np.maximum(np.where(amax > 0, np.frexp(amax)[1] - 1 + 127, 0) - down, 1)
    scale = np.exp2(byte - 127.0)
    codes = (blocks / scale).astype(np.float32).astype(dtype).astype(np.float64)
    return np.moveaxis((codes * scale).reshape(v.shape), -1, axis)


WIDE = False


def mx_kscale(k):
    if not WIDE:
        return np.ones(k)
    levels = np.array([10, -10, 5, -5, 0])
    a = np.random.permutation(np.resize(levels, k // 512 * 4)).reshape(k // 512, 4)
    idx = np.arange(k)
    return np.exp2(a[idx // 512, idx % 128 // 32])


BF16 = ml_dtypes.bfloat16


def bf(x):
    return np.asarray(x, np.float32).astype(BF16)


def f64(x):
    return np.asarray(x).astype(np.float64)


E2M1 = np.array([0.0, 0.5, 1.0, 1.5, 2.0, 3.0, 4.0, 6.0, -0.0, -0.5, -1.0, -1.5, -2.0, -3.0, -4.0, -6.0])


def pack_weight(w, fmt):
    k, n = w.shape
    w = f64(bf(w)).reshape(k // 32, 32, n)
    amax = np.abs(w).max(1)
    if fmt == "e4m3":
        byte = np.frexp(amax)[1] - 1 + 127 - 7
    else:
        mant, ex = np.frexp(amax / 6.0)
        byte = np.where(mant > 0.5, ex, ex - 1) + 127
    byte = np.clip(np.where(amax > 0, byte, 1), 1, 254)
    scaled = (w * np.exp2(127.0 - byte)[:, None, :]).reshape(k, n).astype(np.float32)
    by_word = np.ascontiguousarray(scaled.reshape(k // 512, 128, 4, n).transpose(0, 1, 3, 2))
    if fmt == "e4m3":
        words = by_word.astype(ml_dtypes.float8_e4m3fn).view(np.uint8)
    else:
        c = by_word.astype(ml_dtypes.float4_e2m1fn).view(np.uint8) & 0xF
        words = c[..., 0::2] | (c[..., 1::2] << 4)
    return np.ascontiguousarray(words), np.ascontiguousarray(byte.astype(np.uint8).reshape(k // 512, 16, n))


def unpack_weight(words, scales, fmt):
    g, p, n, _ = words.shape
    if fmt == "e4m3":
        vals = np.ascontiguousarray(words).view(ml_dtypes.float8_e4m3fn).astype(np.float64)
    else:
        nib = np.empty((g, p, n, 4), np.uint8)
        nib[..., 0::2] = words & 0xF
        nib[..., 1::2] = words >> 4
        vals = E2M1[nib]
    vals = vals * np.repeat(np.exp2(scales.astype(np.float64) - 127.0), 8, axis=1)[..., None]
    return vals.transpose(0, 1, 3, 2).reshape(g * 512, n)

def pack4(w):
    words, scales = pack_weight(w, "e2m1")
    return words.reshape(words.shape[0], 128, -1), scales


def unpack4(words, scales):
    return unpack_weight(words.reshape(words.shape[0], 128, -1, 2), scales, "e2m1")


N, S, D, H, O = 4, 256, 1024, 1024, 1024


def elu(v):
    return np.where(v > 0.0, v, np.exp(np.minimum(v, 0.0)) - 1.0)


def setup_inputs():
    s = mx_kscale(D)
    x = bf(np.random.standard_normal((N, S, D)) * s)
    Wk_words, Wk_scales = pack4(np.random.standard_normal((D, H)) / np.sqrt(D) / s[:, None])
    bk = bf(np.random.standard_normal(H) * 0.1)
    Wv_words, Wv_scales = pack4(np.random.standard_normal((D, H)) / np.sqrt(D) / s[:, None])
    bv = bf(np.random.standard_normal(H) * 0.1)
    return {"x": x,
            "Wk_words": Wk_words,
            "Wk_scales": Wk_scales,
            "bk": bk,
            "Wv_words": Wv_words,
            "Wv_scales": Wv_scales,
            "bv": bv}


def reference(x, Wk_words, Wk_scales, bk, Wv_words, Wv_scales, bv):
    xq = mxq(f64(x), 2, "e4m3")
    keyp = (xq @ unpack4(Wk_words, Wk_scales)) + f64(bk)
    value = (xq @ unpack4(Wv_words, Wv_scales)) + f64(bv)
    K = elu(keyp) + 1.0
    KV = np.sum(K * value, axis=1)
    Ksum = np.sum(K, axis=1)
    return KV, Ksum

@@ -1,0 +1,193 @@
+from contextlib import ExitStack
+
+import concourse.mybir as mybir
+from concourse.masks import make_identity
+
+F32 = mybir.dt.float32
+BF16 = mybir.dt.bfloat16
+I32 = mybir.dt.int32
+U32 = mybir.dt.uint32
+U8 = mybir.dt.uint8
+FP8X4 = mybir.dt.float8_e4m3fn_x4
+FP4X4 = mybir.dt.float4_e2m1fn_x4
+ACT = mybir.ActivationFunctionType
+ALU = mybir.AluOpType
+
+P = 128
+BATCH = 4
+SEQ = 256
+FEAT = 1024
+CHAN = 1024
+K_PASS = 512
+GROUPS = FEAT // K_PASS
+CHUNKS = CHAN // P
+N_TOK = 512
+HALVES = BATCH * SEQ // N_TOK
+BATCH_PER_HALF = N_TOK // SEQ
+TILES_PER_BATCH = SEQ // P
+WORDS = FEAT // 2
+
+FLOPS = 2 * BATCH * SEQ * FEAT * 2 * CHAN
+
+
+def tile_linearattention_pa_kernel(
+    tc, x, Wk_words, Wk_scales, bk, Wv_words, Wv_scales, bv, out_0, out_1
+):
+    nc = tc.nc
+    with ExitStack() as ctx:
+        keep = ctx.enter_context(tc.tile_pool(name="keep", bufs=1))
+        work = ctx.enter_context(tc.tile_pool(name="work", bufs=3))
+        psum_t = ctx.enter_context(tc.psum_pool(name="psum_t", bufs=2))
+        psum_mx = ctx.enter_context(tc.psum_pool(name="psum_mx", bufs=3))
+
+        x_sb = keep.tile([P, BATCH, TILES_PER_BATCH, FEAT], BF16, name="x_sb")
+        x_grouped = keep.tile([P, GROUPS, BATCH * SEQ, 4], BF16, name="x_grouped", align_bytes=64)
+        x_codes = keep.tile([P, GROUPS, BATCH * SEQ], U32, name="x_codes", align_bytes=64)
+        x_scales = keep.tile([P, GROUPS, BATCH * SEQ], U8, name="x_scales", align_bytes=64)
+        wk_sb = keep.tile([P, GROUPS, 2 * CHAN], U8, name="wk_sb", align_bytes=64)
+        wv_sb = keep.tile([P, GROUPS, 2 * CHAN], U8, name="wv_sb", align_bytes=64)
+        wk_plane = keep.tile([P, GROUPS, CHAN], U8, name="wk_plane", align_bytes=64)
+        wv_plane = keep.tile([P, GROUPS, CHAN], U8, name="wv_plane", align_bytes=64)
+        ident = keep.tile([P, P], F32, name="ident")
+        bias_rows = keep.tile([P, P], BF16, name="bias_rows")
+        bias_rows32 = keep.tile([P, P], F32, name="bias_rows32")
+        bias_cols = keep.tile([P, 2 * CHUNKS], F32, name="bias_cols")
+        sums = keep.tile([P, P], F32, name="sums")
+        sums_t = keep.tile([P, P], F32, name="sums_t")
+        warm = keep.tile([P, 2], F32, name="warm")
+
+        nc.vector.memset(warm[:], 0.0)
+        nc.scalar.activation(out=warm[:, 1:2], in_=warm[:, 0:1], func=ACT.Exp)
+        nc.vector.memset(bias_rows[:], 0.0)
+        nc.vector.memset(wk_plane[:].bitcast(I32), 0)
+        nc.vector.memset(wv_plane[:].bitcast(I32), 0)
+        nc.vector.memset(sums[:], 0.0)
+        make_identity(nc, ident[:])
+
+        def load_batch(n):
+            nc.sync.dma_start(
+                out=x_sb[:, n, :, :].rearrange("p j k -> p (j k)"),
+                in_=x[n].rearrange("(p j) k -> p (j k)", j=TILES_PER_BATCH),
+            )
+
+        def load_scales(plane, scales):
+            by_r = scales.rearrange("g (q r) n -> r q g n", r=4)
+            for r in range(4):
+                nc.sync.dma_start(out=plane[r:P:32, :, :].bitcast(I32), in_=by_r[r].bitcast(I32))
+
+        def load_words(words_sb, words):
+            nc.sync.dma_start(
+                out=words_sb[:].bitcast(I32), in_=words.rearrange("g p b -> p g b").bitcast(I32)
+            )
+
+        nc.scalar.dma_start(out=bias_rows[0:CHUNKS, :], in_=bk.rearrange("(c h) -> c h", h=P))
+        nc.scalar.dma_start(
+            out=bias_rows[CHUNKS : 2 * CHUNKS, :], in_=bv.rearrange("(c h) -> c h", h=P)
+        )
+        load_batch(0)
+        load_batch(1)
+        load_scales(wk_plane, Wk_scales)
+        load_batch(2)
+        load_batch(3)
+        load_words(wk_sb, Wk_words)
+        load_scales(wv_plane, Wv_scales)
+        load_words(wv_sb, Wv_words)
+
+        nc.vector.tensor_copy(out=bias_rows32[:], in_=bias_rows[:])
+        bias_ps = psum_t.tile([P, N_TOK], F32, tag="tp")
+        nc.tensor.transpose(bias_ps[:, 0:P], bias_rows32[:], ident[:])
+        nc.vector.tensor_copy(out=bias_cols[:], in_=bias_ps[:, 0 : 2 * CHUNKS])
+
+        x_grouped32 = x_grouped[:].bitcast(F32)
+
+        def prepare_half(half):
+            for i in range(BATCH_PER_HALF * TILES_PER_BATCH):
+                n = BATCH_PER_HALF * half + i // TILES_PER_BATCH
+                j = i % TILES_PER_BATCH
+                col = n * SEQ + j * P
+                x_words = x_sb[:, n, j, :].bitcast(F32)
+                tp = psum_t.tile([P, GROUPS, 2, P], F32, tag="tp")
+                for g in range(GROUPS):
+                    for u in range(2):
+                        first = g * (WORDS // GROUPS) + u
+                        last = (g + 1) * (WORDS // GROUPS)
+                        nc.tensor.transpose(tp[:, g, u, :], x_words[:, first:last:2], ident[:])
+                dst = x_grouped32[:, :, col : col + P, :]
+                src = tp[:].rearrange("p g u t -> p g t u")
+                if i % 2 == 0:
+                    nc.vector.tensor_copy(out=dst, in_=src)
+                else:
+                    nc.scalar.copy(out=dst, in_=src)
+            cols = slice(half * N_TOK, (half + 1) * N_TOK)
+            for g in range(GROUPS):
+                nc.vector.quantize_mx(
+                    out=x_codes[:, g, cols].bitcast(FP8X4),
+                    scales=x_scales[:, g, cols],
+                    in_=x_grouped[:, g, cols, :].rearrange("p t f -> p (t f)"),
+                )
+
+        def product(acc, words_sb, plane, half, c):
+            cols = slice(half * N_TOK, (half + 1) * N_TOK)
+            for g in range(GROUPS):
+                nc.tensor.matmul_mx(
+                    out=acc[:],
+                    lhsT=words_sb[:, g, 2 * P * c : 2 * P * (c + 1)].bitcast(FP4X4),
+                    lhsT_scale=plane[:, g, P * c : P * (c + 1)],
+                    rhs=x_codes[:, g, cols].bitcast(FP8X4),
+                    rhs_scale=x_scales[:, g, cols],
+                    start=(g == 0),
+                    stop=(g == GROUPS - 1),
+                )
+
+        def unit(half, c):
+            keyp = psum_mx.tile([P, N_TOK], F32, tag="keyp")
+            product(keyp, wk_sb, wk_plane, half, c)
+            value = psum_mx.tile([P, N_TOK], F32, tag="value")
+            product(value, wv_sb, wv_plane, half, c)
+            bk_col = bias_cols[:, c : c + 1]
+            bv_col = bias_cols[:, CHUNKS + c : CHUNKS + c + 1]
+            expv = work.tile([P, N_TOK], F32, tag="expv")
+            nc.scalar.activation(out=expv[:], in_=keyp[:], func=ACT.Exp, bias=bk_col, scale=1.0)
+            reluv = work.tile([P, N_TOK], F32, tag="reluv")
+            nc.scalar.activation(out=reluv[:], in_=keyp[:], func=ACT.Relu, bias=bk_col, scale=1.0)
+            kmat = work.tile([P, N_TOK], F32, tag="kmat")
+            prod = work.tile([P, N_TOK], F32, tag="prod")
+            for b in range(BATCH_PER_HALF):
+                s = slice(b * SEQ, (b + 1) * SEQ)
+                ksum_col = BATCH * CHUNKS + CHUNKS * (BATCH_PER_HALF * half + b) + c
+                nc.vector.scalar_tensor_tensor(
+                    out=kmat[:, s],
+                    in0=expv[:, s],
+                    scalar=1.0,
+                    in1=reluv[:, s],
+                    op0=ALU.min,
+                    op1=ALU.add,
+                    accum_out=sums[:, ksum_col : ksum_col + 1],
+                )
+            for b in range(BATCH_PER_HALF):
+                s = slice(b * SEQ, (b + 1) * SEQ)
+                kv_col = CHUNKS * (BATCH_PER_HALF * half + b) + c
+                nc.vector.scalar_tensor_tensor(
+                    out=prod[:, s],
+                    in0=value[:, s],
+                    scalar=bv_col,
+                    in1=kmat[:, s],
+                    op0=ALU.add,
+                    op1=ALU.mult,
+                    accum_out=sums[:, kv_col : kv_col + 1],
+                )
+
+        for half in range(HALVES):
+            prepare_half(half)
+        for half in range(HALVES):
+            for c in range(CHUNKS):
+                unit(half, c)
+
+        sums_ps = psum_t.tile([P, N_TOK], F32, tag="tp")
+        nc.tensor.transpose(sums_ps[:, 0:P], sums[:], ident[:])
+        rows = BATCH * CHUNKS
+        nc.vector.tensor_copy(out=sums_t[0 : 2 * rows, :], in_=sums_ps[0 : 2 * rows, 0:P])
+        nc.sync.dma_start(out=out_0.rearrange("n (c h) -> (n c) h", h=P), in_=sums_t[0:rows, :])
+        nc.scalar.dma_start(
+            out=out_1.rearrange("n (c h) -> (n c) h", h=P), in_=sums_t[rows : 2 * rows, :]
+        )

@@ -26,6 +26,12 @@ HALVES = BATCH * SEQ // N_TOK
 BATCH_PER_HALF = N_TOK // SEQ
 TILES_PER_BATCH = SEQ // P
 WORDS = FEAT // 2
+TOKEN_TILES = BATCH * SEQ // P
+PSUM_BANKS = 8
+UNITS = HALVES * CHUNKS
+W_PARTS = 2
+PART_BYTES = 2 * CHAN // W_PARTS
+CHUNKS_PER_PART = CHUNKS // W_PARTS
 
 FLOPS = 2 * BATCH * SEQ * FEAT * 2 * CHAN
 
@@ -36,16 +42,16 @@ def tile_linearattention_pa_kernel(
     nc = tc.nc
     with ExitStack() as ctx:
         keep = ctx.enter_context(tc.tile_pool(name="keep", bufs=1))
-        work = ctx.enter_context(tc.tile_pool(name="work", bufs=3))
-        psum_t = ctx.enter_context(tc.psum_pool(name="psum_t", bufs=2))
-        psum_mx = ctx.enter_context(tc.psum_pool(name="psum_mx", bufs=3))
+        work = ctx.enter_context(tc.tile_pool(name="work", bufs=4))
+        psum = ctx.enter_context(tc.psum_pool(name="psum", bufs=PSUM_BANKS))
+        ctx.enter_context(tc.manual_schedule())
 
         x_sb = keep.tile([P, BATCH, TILES_PER_BATCH, FEAT], BF16, name="x_sb")
-        x_grouped = keep.tile([P, GROUPS, BATCH * SEQ, 4], BF16, name="x_grouped", align_bytes=64)
+        x_grouped = keep.tile([P, TOKEN_TILES, GROUPS, P, 4], BF16, name="x_grouped", align_bytes=64)
         x_codes = keep.tile([P, GROUPS, BATCH * SEQ], U32, name="x_codes", align_bytes=64)
         x_scales = keep.tile([P, GROUPS, BATCH * SEQ], U8, name="x_scales", align_bytes=64)
-        wk_sb = keep.tile([P, GROUPS, 2 * CHAN], U8, name="wk_sb", align_bytes=64)
-        wv_sb = keep.tile([P, GROUPS, 2 * CHAN], U8, name="wv_sb", align_bytes=64)
+        wk_sb = keep.tile([P, W_PARTS, GROUPS, PART_BYTES], U8, name="wk_sb", align_bytes=64)
+        wv_sb = keep.tile([P, W_PARTS, GROUPS, PART_BYTES], U8, name="wv_sb", align_bytes=64)
         wk_plane = keep.tile([P, GROUPS, CHAN], U8, name="wk_plane", align_bytes=64)
         wv_plane = keep.tile([P, GROUPS, CHAN], U8, name="wv_plane", align_bytes=64)
         ident = keep.tile([P, P], F32, name="ident")
@@ -75,9 +81,11 @@ def tile_linearattention_pa_kernel(
             for r in range(4):
                 nc.sync.dma_start(out=plane[r:P:32, :, :].bitcast(I32), in_=by_r[r].bitcast(I32))
 
-        def load_words(words_sb, words):
+        def load_words(words_sb, words, part):
+            b = slice(part * PART_BYTES, (part + 1) * PART_BYTES)
             nc.sync.dma_start(
-                out=words_sb[:].bitcast(I32), in_=words.rearrange("g p b -> p g b").bitcast(I32)
+                out=words_sb[:, part, :, :].bitcast(I32),
+                in_=words.rearrange("g p b -> p g b")[:, :, b].bitcast(I32),
             )
 
         nc.scalar.dma_start(out=bias_rows[0:CHUNKS, :], in_=bk.rearrange("(c h) -> c h", h=P))
@@ -89,49 +97,54 @@ def tile_linearattention_pa_kernel(
         load_scales(wk_plane, Wk_scales)
         load_batch(2)
         load_batch(3)
-        load_words(wk_sb, Wk_words)
+        load_words(wk_sb, Wk_words, 0)
         load_scales(wv_plane, Wv_scales)
-        load_words(wv_sb, Wv_words)
+        load_words(wv_sb, Wv_words, 0)
+        load_words(wk_sb, Wk_words, 1)
+        load_words(wv_sb, Wv_words, 1)
 
         nc.vector.tensor_copy(out=bias_rows32[:], in_=bias_rows[:])
-        bias_ps = psum_t.tile([P, N_TOK], F32, tag="tp")
+        bias_ps = psum.tile([P, N_TOK], F32, tag="bank")
         nc.tensor.transpose(bias_ps[:, 0:P], bias_rows32[:], ident[:])
         nc.vector.tensor_copy(out=bias_cols[:], in_=bias_ps[:, 0 : 2 * CHUNKS])
 
         x_grouped32 = x_grouped[:].bitcast(F32)
 
-        def prepare_half(half):
-            for i in range(BATCH_PER_HALF * TILES_PER_BATCH):
-                n = BATCH_PER_HALF * half + i // TILES_PER_BATCH
-                j = i % TILES_PER_BATCH
-                col = n * SEQ + j * P
-                x_words = x_sb[:, n, j, :].bitcast(F32)
-                tp = psum_t.tile([P, GROUPS, 2, P], F32, tag="tp")
-                for g in range(GROUPS):
-                    for u in range(2):
-                        first = g * (WORDS // GROUPS) + u
-                        last = (g + 1) * (WORDS // GROUPS)
-                        nc.tensor.transpose(tp[:, g, u, :], x_words[:, first:last:2], ident[:])
-                dst = x_grouped32[:, :, col : col + P, :]
-                src = tp[:].rearrange("p g u t -> p g t u")
-                if i % 2 == 0:
-                    nc.vector.tensor_copy(out=dst, in_=src)
-                else:
-                    nc.scalar.copy(out=dst, in_=src)
-            cols = slice(half * N_TOK, (half + 1) * N_TOK)
+        def transpose_tile(i):
+            n = i // TILES_PER_BATCH
+            j = i % TILES_PER_BATCH
+            x_words = x_sb[:, n, j, :].bitcast(F32)
+            bank = psum.tile([P, N_TOK], F32, tag="bank")
+            turned = bank[:].rearrange("p (g u t) -> p g u t", g=GROUPS, u=2)
+            for g in range(GROUPS):
+                for u in range(2):
+                    first = g * (WORDS // GROUPS) + u
+                    last = (g + 1) * (WORDS // GROUPS)
+                    nc.tensor.transpose(turned[:, g, u, :], x_words[:, first:last:2], ident[:])
+            dst = x_grouped32[:, i, :, :, :]
+            src = turned.rearrange("p g u t -> p g t u")
+            if i % 2 == 0:
+                nc.vector.tensor_copy(out=dst, in_=src)
+            else:
+                nc.scalar.copy(out=dst, in_=src)
+
+        def quantise_tile(i):
+            cols = slice(i * P, (i + 1) * P)
             for g in range(GROUPS):
                 nc.vector.quantize_mx(
                     out=x_codes[:, g, cols].bitcast(FP8X4),
                     scales=x_scales[:, g, cols],
-                    in_=x_grouped[:, g, cols, :].rearrange("p t f -> p (t f)"),
+                    in_=x_grouped[:, i, g, :, :].rearrange("p t f -> p (t f)"),
                 )
 
         def product(acc, words_sb, plane, half, c):
             cols = slice(half * N_TOK, (half + 1) * N_TOK)
+            part = c // CHUNKS_PER_PART
+            first = 2 * P * (c % CHUNKS_PER_PART)
             for g in range(GROUPS):
                 nc.tensor.matmul_mx(
                     out=acc[:],
-                    lhsT=words_sb[:, g, 2 * P * c : 2 * P * (c + 1)].bitcast(FP4X4),
+                    lhsT=words_sb[:, part, g, first : first + 2 * P].bitcast(FP4X4),
                     lhsT_scale=plane[:, g, P * c : P * (c + 1)],
                     rhs=x_codes[:, g, cols].bitcast(FP8X4),
                     rhs_scale=x_scales[:, g, cols],
@@ -139,19 +152,19 @@ def tile_linearattention_pa_kernel(
                     stop=(g == GROUPS - 1),
                 )
 
-        def unit(half, c):
-            keyp = psum_mx.tile([P, N_TOK], F32, tag="keyp")
+        def make_k(i):
+            half = i // CHUNKS
+            c = i % CHUNKS
+            keyp = psum.tile([P, N_TOK], F32, tag="bank")
             product(keyp, wk_sb, wk_plane, half, c)
-            value = psum_mx.tile([P, N_TOK], F32, tag="value")
+            value = psum.tile([P, N_TOK], F32, tag="bank")
             product(value, wv_sb, wv_plane, half, c)
             bk_col = bias_cols[:, c : c + 1]
-            bv_col = bias_cols[:, CHUNKS + c : CHUNKS + c + 1]
             expv = work.tile([P, N_TOK], F32, tag="expv")
             nc.scalar.activation(out=expv[:], in_=keyp[:], func=ACT.Exp, bias=bk_col, scale=1.0)
             reluv = work.tile([P, N_TOK], F32, tag="reluv")
             nc.scalar.activation(out=reluv[:], in_=keyp[:], func=ACT.Relu, bias=bk_col, scale=1.0)
             kmat = work.tile([P, N_TOK], F32, tag="kmat")
-            prod = work.tile([P, N_TOK], F32, tag="prod")
             for b in range(BATCH_PER_HALF):
                 s = slice(b * SEQ, (b + 1) * SEQ)
                 ksum_col = BATCH * CHUNKS + CHUNKS * (BATCH_PER_HALF * half + b) + c
@@ -164,6 +177,13 @@ def tile_linearattention_pa_kernel(
                     op1=ALU.add,
                     accum_out=sums[:, ksum_col : ksum_col + 1],
                 )
+            return value, kmat
+
+        def sum_kv(i, value, kmat):
+            half = i // CHUNKS
+            c = i % CHUNKS
+            bv_col = bias_cols[:, CHUNKS + c : CHUNKS + c + 1]
+            prod = work.tile([P, N_TOK], F32, tag="prod")
             for b in range(BATCH_PER_HALF):
                 s = slice(b * SEQ, (b + 1) * SEQ)
                 kv_col = CHUNKS * (BATCH_PER_HALF * half + b) + c
@@ -177,13 +197,19 @@ def tile_linearattention_pa_kernel(
                     accum_out=sums[:, kv_col : kv_col + 1],
                 )
 
-        for half in range(HALVES):
-            prepare_half(half)
-        for half in range(HALVES):
-            for c in range(CHUNKS):
-                unit(half, c)
+        for i in range(TOKEN_TILES):
+            transpose_tile(i)
+            if i > 0:
+                quantise_tile(i - 1)
+        quantise_tile(TOKEN_TILES - 1)
+        made = {}
+        for i in range(UNITS):
+            made[i] = make_k(i)
+            if i > 0:
+                sum_kv(i - 1, *made[i - 1])
+        sum_kv(UNITS - 1, *made[UNITS - 1])
 
-        sums_ps = psum_t.tile([P, N_TOK], F32, tag="tp")
+        sums_ps = psum.tile([P, N_TOK], F32, tag="bank")
         nc.tensor.transpose(sums_ps[:, 0:P], sums[:], ident[:])
         rows = BATCH * CHUNKS
         nc.vector.tensor_copy(out=sums_t[0 : 2 * rows, :], in_=sums_ps[0 : 2 * rows, 0:P])

@@ -57,7 +57,7 @@ def tile_linearattention_pa_kernel(
         ident = keep.tile([P, P], F32, name="ident")
         bias_rows = keep.tile([P, P], BF16, name="bias_rows")
         bias_rows32 = keep.tile([P, P], F32, name="bias_rows32")
-        bias_cols = keep.tile([P, 2 * CHUNKS], F32, name="bias_cols")
+        bias_cols = keep.tile([P, 3 * CHUNKS], F32, name="bias_cols")
         sums = keep.tile([P, P], F32, name="sums")
         sums_t = keep.tile([P, P], F32, name="sums_t")
         warm = keep.tile([P, 2], F32, name="warm")
@@ -106,7 +106,10 @@ def tile_linearattention_pa_kernel(
         nc.vector.tensor_copy(out=bias_rows32[:], in_=bias_rows[:])
         bias_ps = psum.tile([P, N_TOK], F32, tag="bank")
         nc.tensor.transpose(bias_ps[:, 0:P], bias_rows32[:], ident[:])
-        nc.vector.tensor_copy(out=bias_cols[:], in_=bias_ps[:, 0 : 2 * CHUNKS])
+        nc.vector.tensor_copy(out=bias_cols[:, 0 : 2 * CHUNKS], in_=bias_ps[:, 0 : 2 * CHUNKS])
+        nc.vector.tensor_scalar_add(
+            out=bias_cols[:, 2 * CHUNKS : 3 * CHUNKS], in0=bias_cols[:, 0:CHUNKS], scalar1=1.0
+        )
 
         x_grouped32 = x_grouped[:].bitcast(F32)
 
@@ -152,45 +155,61 @@ def tile_linearattention_pa_kernel(
                     stop=(g == GROUPS - 1),
                 )
 
-        def make_k(i):
+        banks = {}
+        tiles = {}
+
+        def start_unit(i):
             half = i // CHUNKS
             c = i % CHUNKS
             keyp = psum.tile([P, N_TOK], F32, tag="bank")
             product(keyp, wk_sb, wk_plane, half, c)
             value = psum.tile([P, N_TOK], F32, tag="bank")
             product(value, wv_sb, wv_plane, half, c)
-            bk_col = bias_cols[:, c : c + 1]
             expv = work.tile([P, N_TOK], F32, tag="expv")
-            nc.scalar.activation(out=expv[:], in_=keyp[:], func=ACT.Exp, bias=bk_col, scale=1.0)
-            reluv = work.tile([P, N_TOK], F32, tag="reluv")
-            nc.scalar.activation(out=reluv[:], in_=keyp[:], func=ACT.Relu, bias=bk_col, scale=1.0)
-            kmat = work.tile([P, N_TOK], F32, tag="kmat")
-            for b in range(BATCH_PER_HALF):
-                s = slice(b * SEQ, (b + 1) * SEQ)
-                ksum_col = BATCH * CHUNKS + CHUNKS * (BATCH_PER_HALF * half + b) + c
-                nc.vector.scalar_tensor_tensor(
-                    out=kmat[:, s],
-                    in0=expv[:, s],
-                    scalar=1.0,
-                    in1=reluv[:, s],
-                    op0=ALU.min,
-                    op1=ALU.add,
-                    accum_out=sums[:, ksum_col : ksum_col + 1],
-                )
-            return value, kmat
+            nc.scalar.activation(
+                out=expv[:], in_=keyp[:], func=ACT.Exp, bias=bias_cols[:, c : c + 1], scale=1.0
+            )
+            capped = work.tile([P, N_TOK], F32, tag="capped")
+            nc.gpsimd.tensor_scalar(
+                out=capped[:], in0=expv[:], scalar1=1.0, scalar2=0.0, op0=ALU.min, op1=ALU.max
+            )
+            banks[i] = (keyp, value)
+            tiles[i] = capped
 
-        def sum_kv(i, value, kmat):
+        def make_k(i):
+            c = i % CHUNKS
+            kmat = work.tile([P, N_TOK], F32, tag="kmat")
+            nc.vector.scalar_tensor_tensor(
+                out=kmat[:],
+                in0=banks[i][0][:],
+                scalar=bias_cols[:, 2 * CHUNKS + c : 2 * CHUNKS + c + 1],
+                in1=tiles[i][:],
+                op0=ALU.add,
+                op1=ALU.max,
+            )
+            tiles[i] = kmat
+
+        def sum_unit(i):
             half = i // CHUNKS
             c = i % CHUNKS
-            bv_col = bias_cols[:, CHUNKS + c : CHUNKS + c + 1]
+            kmat = tiles[i]
+            value = banks[i][1]
+            copy_of_k = work.tile([P, N_TOK], F32, tag="copy_of_k")
             prod = work.tile([P, N_TOK], F32, tag="prod")
             for b in range(BATCH_PER_HALF):
                 s = slice(b * SEQ, (b + 1) * SEQ)
                 kv_col = CHUNKS * (BATCH_PER_HALF * half + b) + c
+                ksum_col = BATCH * CHUNKS + kv_col
+                nc.scalar.activation(
+                    out=copy_of_k[:, s],
+                    in_=kmat[:, s],
+                    func=ACT.Copy,
+                    accum_out=sums[:, ksum_col : ksum_col + 1],
+                )
                 nc.vector.scalar_tensor_tensor(
                     out=prod[:, s],
                     in0=value[:, s],
-                    scalar=bv_col,
+                    scalar=bias_cols[:, CHUNKS + c : CHUNKS + c + 1],
                     in1=kmat[:, s],
                     op0=ALU.add,
                     op1=ALU.mult,
@@ -202,12 +221,13 @@ def tile_linearattention_pa_kernel(
             if i > 0:
                 quantise_tile(i - 1)
         quantise_tile(TOKEN_TILES - 1)
-        made = {}
-        for i in range(UNITS):
-            made[i] = make_k(i)
-            if i > 0:
-                sum_kv(i - 1, *made[i - 1])
-        sum_kv(UNITS - 1, *made[UNITS - 1])
+        for step in range(UNITS + 2):
+            if step < UNITS:
+                start_unit(step)
+            if 1 <= step <= UNITS:
+                make_k(step - 1)
+            if step >= 2:
+                sum_unit(step - 2)
 
         sums_ps = psum.tile([P, N_TOK], F32, tag="bank")
         nc.tensor.transpose(sums_ps[:, 0:P], sums[:], ident[:])

@@ -163,8 +163,6 @@ def tile_linearattention_pa_kernel(
             c = i % CHUNKS
             keyp = psum.tile([P, N_TOK], F32, tag="bank")
             product(keyp, wk_sb, wk_plane, half, c)
-            value = psum.tile([P, N_TOK], F32, tag="bank")
-            product(value, wv_sb, wv_plane, half, c)
             expv = work.tile([P, N_TOK], F32, tag="expv")
             nc.scalar.activation(
                 out=expv[:], in_=keyp[:], func=ACT.Exp, bias=bias_cols[:, c : c + 1], scale=1.0
@@ -173,27 +171,31 @@ def tile_linearattention_pa_kernel(
             nc.gpsimd.tensor_scalar(
                 out=capped[:], in0=expv[:], scalar1=1.0, scalar2=0.0, op0=ALU.min, op1=ALU.max
             )
-            banks[i] = (keyp, value)
+            banks[i] = keyp
             tiles[i] = capped
 
         def make_k(i):
+            half = i // CHUNKS
             c = i % CHUNKS
+            value = psum.tile([P, N_TOK], F32, tag="bank")
+            product(value, wv_sb, wv_plane, half, c)
             kmat = work.tile([P, N_TOK], F32, tag="kmat")
             nc.vector.scalar_tensor_tensor(
                 out=kmat[:],
-                in0=banks[i][0][:],
+                in0=banks[i][:],
                 scalar=bias_cols[:, 2 * CHUNKS + c : 2 * CHUNKS + c + 1],
                 in1=tiles[i][:],
                 op0=ALU.add,
                 op1=ALU.max,
             )
+            banks[i] = value
             tiles[i] = kmat
 
         def sum_unit(i):
             half = i // CHUNKS
             c = i % CHUNKS
             kmat = tiles[i]
-            value = banks[i][1]
+            value = banks[i]
             copy_of_k = work.tile([P, N_TOK], F32, tag="copy_of_k")
             prod = work.tile([P, N_TOK], F32, tag="prod")
             for b in range(BATCH_PER_HALF):

@@ -33,6 +33,10 @@ W_PARTS = 2
 PART_BYTES = 2 * CHAN // W_PARTS
 CHUNKS_PER_PART = CHUNKS // W_PARTS
 
+PREPS = BATCH * GROUPS
+VECTOR_COPIES_EVERY = 4
+BIAS_AFTER_BATCH = 1
+
 FLOPS = 2 * BATCH * SEQ * FEAT * 2 * CHAN
 
 
@@ -47,7 +51,7 @@ def tile_linearattention_pa_kernel(
         ctx.enter_context(tc.manual_schedule())
 
         x_sb = keep.tile([P, BATCH, TILES_PER_BATCH, FEAT], BF16, name="x_sb")
-        x_grouped = keep.tile([P, TOKEN_TILES, GROUPS, P, 4], BF16, name="x_grouped", align_bytes=64)
+        x_grouped = keep.tile([P, BATCH, GROUPS, SEQ, 4], BF16, name="x_grouped", align_bytes=64)
         x_codes = keep.tile([P, GROUPS, BATCH * SEQ], U32, name="x_codes", align_bytes=64)
         x_scales = keep.tile([P, GROUPS, BATCH * SEQ], U8, name="x_scales", align_bytes=64)
         wk_sb = keep.tile([P, W_PARTS, GROUPS, PART_BYTES], U8, name="wk_sb", align_bytes=64)
@@ -71,10 +75,11 @@ def tile_linearattention_pa_kernel(
         make_identity(nc, ident[:])
 
         def load_batch(n):
-            nc.sync.dma_start(
-                out=x_sb[:, n, :, :].rearrange("p j k -> p (j k)"),
-                in_=x[n].rearrange("(p j) k -> p (j k)", j=TILES_PER_BATCH),
-            )
+            for j in range(TILES_PER_BATCH):
+                nc.sync.dma_start(
+                    out=x_sb[:, n, j, :],
+                    in_=x[n].rearrange("(p j) k -> p j k", j=TILES_PER_BATCH)[:, j, :],
+                )
 
         def load_scales(plane, scales):
             by_r = scales.rearrange("g (q r) n -> r q g n", r=4)
@@ -94,51 +99,65 @@ def tile_linearattention_pa_kernel(
         )
         load_batch(0)
         load_batch(1)
-        load_scales(wk_plane, Wk_scales)
         load_batch(2)
         load_batch(3)
+        load_scales(wk_plane, Wk_scales)
         load_words(wk_sb, Wk_words, 0)
         load_scales(wv_plane, Wv_scales)
         load_words(wv_sb, Wv_words, 0)
         load_words(wk_sb, Wk_words, 1)
         load_words(wv_sb, Wv_words, 1)
 
-        nc.vector.tensor_copy(out=bias_rows32[:], in_=bias_rows[:])
-        bias_ps = psum.tile([P, N_TOK], F32, tag="bank")
-        nc.tensor.transpose(bias_ps[:, 0:P], bias_rows32[:], ident[:])
-        nc.vector.tensor_copy(out=bias_cols[:, 0 : 2 * CHUNKS], in_=bias_ps[:, 0 : 2 * CHUNKS])
-        nc.vector.tensor_scalar_add(
-            out=bias_cols[:, 2 * CHUNKS : 3 * CHUNKS], in0=bias_cols[:, 0:CHUNKS], scalar1=1.0
-        )
+        bias_banks = []
+
+        def turn_biases():
+            nc.vector.tensor_copy(out=bias_rows32[:], in_=bias_rows[:])
+            bias_ps = psum.tile([P, N_TOK], F32, tag="bank")
+            nc.tensor.transpose(bias_ps[:, 0:P], bias_rows32[:], ident[:])
+            bias_banks.append(bias_ps)
+
+        def keep_biases():
+            bias_ps = bias_banks[0]
+            nc.vector.tensor_copy(out=bias_cols[:, 0 : 2 * CHUNKS], in_=bias_ps[:, 0 : 2 * CHUNKS])
+            nc.vector.tensor_scalar_add(
+                out=bias_cols[:, 2 * CHUNKS : 3 * CHUNKS], in0=bias_cols[:, 0:CHUNKS], scalar1=1.0
+            )
 
         x_grouped32 = x_grouped[:].bitcast(F32)
 
-        def transpose_tile(i):
-            n = i // TILES_PER_BATCH
-            j = i % TILES_PER_BATCH
-            x_words = x_sb[:, n, j, :].bitcast(F32)
-            bank = psum.tile([P, N_TOK], F32, tag="bank")
-            turned = bank[:].rearrange("p (g u t) -> p g u t", g=GROUPS, u=2)
+        def turn_batch(n):
+            pieces = []
             for g in range(GROUPS):
-                for u in range(2):
-                    first = g * (WORDS // GROUPS) + u
-                    last = (g + 1) * (WORDS // GROUPS)
-                    nc.tensor.transpose(turned[:, g, u, :], x_words[:, first:last:2], ident[:])
-            dst = x_grouped32[:, i, :, :, :]
-            src = turned.rearrange("p g u t -> p g t u")
-            if i % 2 == 0:
-                nc.vector.tensor_copy(out=dst, in_=src)
-            else:
-                nc.scalar.copy(out=dst, in_=src)
-
-        def quantise_tile(i):
-            cols = slice(i * P, (i + 1) * P)
+                bank = psum.tile([P, N_TOK], F32, tag="bank")
+                pieces.append(bank[:].rearrange("p (j u t) -> p j u t", j=TILES_PER_BATCH, u=2))
+            for j in range(TILES_PER_BATCH):
+                x_words = x_sb[:, n, j, :].bitcast(F32)
+                for g in range(GROUPS):
+                    for u in range(2):
+                        first = g * (WORDS // GROUPS) + u
+                        last = (g + 1) * (WORDS // GROUPS)
+                        nc.tensor.transpose(
+                            pieces[g][:, j, u, :], x_words[:, first:last:2], ident[:]
+                        )
             for g in range(GROUPS):
-                nc.vector.quantize_mx(
-                    out=x_codes[:, g, cols].bitcast(FP8X4),
-                    scales=x_scales[:, g, cols],
-                    in_=x_grouped[:, i, g, :, :].rearrange("p t f -> p (t f)"),
+                dst = x_grouped32[:, n, g, :, :].rearrange(
+                    "p (j t) u -> p j t u", j=TILES_PER_BATCH
                 )
+                src = pieces[g].rearrange("p j u t -> p j t u")
+                if (GROUPS * n + g) % VECTOR_COPIES_EVERY == 0:
+                    nc.vector.tensor_copy(out=dst, in_=src)
+                else:
+                    nc.scalar.copy(out=dst, in_=src)
+
+        def quantise_piece(i):
+            n = i // GROUPS
+            g = i % GROUPS
+            cols = slice(n * SEQ, (n + 1) * SEQ)
+            nc.vector.quantize_mx(
+                out=x_codes[:, g, cols].bitcast(FP8X4),
+                scales=x_scales[:, g, cols],
+                in_=x_grouped[:, n, g, :, :].rearrange("p t f -> p (t f)"),
+            )
 
         def product(acc, words_sb, plane, half, c):
             cols = slice(half * N_TOK, (half + 1) * N_TOK)
@@ -218,11 +237,17 @@ def tile_linearattention_pa_kernel(
                     accum_out=sums[:, kv_col : kv_col + 1],
                 )
 
-        for i in range(TOKEN_TILES):
-            transpose_tile(i)
-            if i > 0:
-                quantise_tile(i - 1)
-        quantise_tile(TOKEN_TILES - 1)
+        for n in range(BATCH):
+            turn_batch(n)
+            if n > 0:
+                for g in range(GROUPS):
+                    quantise_piece(GROUPS * (n - 1) + g)
+            if n == BIAS_AFTER_BATCH:
+                turn_biases()
+            if n == BIAS_AFTER_BATCH + 1:
+                keep_biases()
+        for g in range(GROUPS):
+            quantise_piece(GROUPS * (BATCH - 1) + g)
         for step in range(UNITS + 2):
             if step < UNITS:
                 start_unit(step)

@@ -187,9 +187,12 @@ def tile_linearattention_pa_kernel(
                 out=expv[:], in_=keyp[:], func=ACT.Exp, bias=bias_cols[:, c : c + 1], scale=1.0
             )
             capped = work.tile([P, N_TOK], F32, tag="capped")
-            nc.gpsimd.tensor_scalar(
-                out=capped[:], in0=expv[:], scalar1=1.0, scalar2=0.0, op0=ALU.min, op1=ALU.max
-            )
+            if i == 0:
+                nc.vector.tensor_scalar_min(out=capped[:], in0=expv[:], scalar1=1.0)
+            else:
+                nc.gpsimd.tensor_scalar(
+                    out=capped[:], in0=expv[:], scalar1=1.0, scalar2=0.0, op0=ALU.min, op1=ALU.max
+                )
             banks[i] = keyp
             tiles[i] = capped
 

@@ -25,7 +25,6 @@ N_TOK = 512
 HALVES = BATCH * SEQ // N_TOK
 BATCH_PER_HALF = N_TOK // SEQ
 TILES_PER_BATCH = SEQ // P
-WORDS = FEAT // 2
 TOKEN_TILES = BATCH * SEQ // P
 PSUM_BANKS = 8
 UNITS = HALVES * CHUNKS
@@ -33,8 +32,11 @@ W_PARTS = 2
 PART_BYTES = 2 * CHAN // W_PARTS
 CHUNKS_PER_PART = CHUNKS // W_PARTS
 
+SUM_COLS = BATCH * CHUNKS
+QUAD = 32
+
 PREPS = BATCH * GROUPS
-VECTOR_COPIES_EVERY = 4
+VECTOR_COPIES = (PREPS - 1,)
 BIAS_AFTER_BATCH = 1
 
 FLOPS = 2 * BATCH * SEQ * FEAT * 2 * CHAN
@@ -51,6 +53,9 @@ def tile_linearattention_pa_kernel(
         ctx.enter_context(tc.manual_schedule())
 
         x_sb = keep.tile([P, BATCH, TILES_PER_BATCH, FEAT], BF16, name="x_sb")
+        x_sorted = keep.tile(
+            [P, BATCH, TILES_PER_BATCH, GROUPS, 2, P], F32, name="x_sorted", align_bytes=64
+        )
         x_grouped = keep.tile([P, BATCH, GROUPS, SEQ, 4], BF16, name="x_grouped", align_bytes=64)
         x_codes = keep.tile([P, GROUPS, BATCH * SEQ], U32, name="x_codes", align_bytes=64)
         x_scales = keep.tile([P, GROUPS, BATCH * SEQ], U8, name="x_scales", align_bytes=64)
@@ -62,8 +67,10 @@ def tile_linearattention_pa_kernel(
         bias_rows = keep.tile([P, P], BF16, name="bias_rows")
         bias_rows32 = keep.tile([P, P], F32, name="bias_rows32")
         bias_cols = keep.tile([P, 3 * CHUNKS], F32, name="bias_cols")
-        sums = keep.tile([P, P], F32, name="sums")
-        sums_t = keep.tile([P, P], F32, name="sums_t")
+        kv_sums = keep.tile([P, SUM_COLS], F32, name="kv_sums", align_bytes=64)
+        k_sums = keep.tile([P, SUM_COLS], F32, name="k_sums", align_bytes=64)
+        kv_turned = keep.tile([P, SUM_COLS], F32, name="kv_turned", align_bytes=64)
+        k_turned = keep.tile([P, SUM_COLS], F32, name="k_turned", align_bytes=64)
         warm = keep.tile([P, 2], F32, name="warm")
 
         nc.vector.memset(warm[:], 0.0)
@@ -71,7 +78,6 @@ def tile_linearattention_pa_kernel(
         nc.vector.memset(bias_rows[:], 0.0)
         nc.vector.memset(wk_plane[:].bitcast(I32), 0)
         nc.vector.memset(wv_plane[:].bitcast(I32), 0)
-        nc.vector.memset(sums[:], 0.0)
         make_identity(nc, ident[:])
 
         def load_batch(n):
@@ -125,26 +131,32 @@ def tile_linearattention_pa_kernel(
 
         x_grouped32 = x_grouped[:].bitcast(F32)
 
+        def sort_words(n):
+            for j in range(TILES_PER_BATCH):
+                nc.vector.tensor_copy(
+                    out=x_sorted[:, n, j, :, :, :],
+                    in_=x_sb[:, n, j, :]
+                    .bitcast(F32)
+                    .rearrange("p (g i u) -> p g u i", g=GROUPS, u=2),
+                )
+
         def turn_batch(n):
             pieces = []
             for g in range(GROUPS):
                 bank = psum.tile([P, N_TOK], F32, tag="bank")
                 pieces.append(bank[:].rearrange("p (j u t) -> p j u t", j=TILES_PER_BATCH, u=2))
             for j in range(TILES_PER_BATCH):
-                x_words = x_sb[:, n, j, :].bitcast(F32)
                 for g in range(GROUPS):
                     for u in range(2):
-                        first = g * (WORDS // GROUPS) + u
-                        last = (g + 1) * (WORDS // GROUPS)
                         nc.tensor.transpose(
-                            pieces[g][:, j, u, :], x_words[:, first:last:2], ident[:]
+                            pieces[g][:, j, u, :], x_sorted[:, n, j, g, u, :], ident[:]
                         )
             for g in range(GROUPS):
                 dst = x_grouped32[:, n, g, :, :].rearrange(
                     "p (j t) u -> p j t u", j=TILES_PER_BATCH
                 )
                 src = pieces[g].rearrange("p j u t -> p j t u")
-                if (GROUPS * n + g) % VECTOR_COPIES_EVERY == 0:
+                if GROUPS * n + g in VECTOR_COPIES:
                     nc.vector.tensor_copy(out=dst, in_=src)
                 else:
                     nc.scalar.copy(out=dst, in_=src)
@@ -222,13 +234,12 @@ def tile_linearattention_pa_kernel(
             prod = work.tile([P, N_TOK], F32, tag="prod")
             for b in range(BATCH_PER_HALF):
                 s = slice(b * SEQ, (b + 1) * SEQ)
-                kv_col = CHUNKS * (BATCH_PER_HALF * half + b) + c
-                ksum_col = BATCH * CHUNKS + kv_col
+                col = CHUNKS * (BATCH_PER_HALF * half + b) + c
                 nc.scalar.activation(
                     out=copy_of_k[:, s],
                     in_=kmat[:, s],
                     func=ACT.Copy,
-                    accum_out=sums[:, ksum_col : ksum_col + 1],
+                    accum_out=k_sums[:, col : col + 1],
                 )
                 nc.vector.scalar_tensor_tensor(
                     out=prod[:, s],
@@ -237,10 +248,13 @@ def tile_linearattention_pa_kernel(
                     in1=kmat[:, s],
                     op0=ALU.add,
                     op1=ALU.mult,
-                    accum_out=sums[:, kv_col : kv_col + 1],
+                    accum_out=kv_sums[:, col : col + 1],
                 )
 
+        sort_words(0)
         for n in range(BATCH):
+            if n + 1 < BATCH:
+                sort_words(n + 1)
             turn_batch(n)
             if n > 0:
                 for g in range(GROUPS):
@@ -259,11 +273,15 @@ def tile_linearattention_pa_kernel(
             if step >= 2:
                 sum_unit(step - 2)
 
-        sums_ps = psum.tile([P, N_TOK], F32, tag="bank")
-        nc.tensor.transpose(sums_ps[:, 0:P], sums[:], ident[:])
-        rows = BATCH * CHUNKS
-        nc.vector.tensor_copy(out=sums_t[0 : 2 * rows, :], in_=sums_ps[0 : 2 * rows, 0:P])
-        nc.sync.dma_start(out=out_0.rearrange("n (c h) -> (n c) h", h=P), in_=sums_t[0:rows, :])
-        nc.scalar.dma_start(
-            out=out_1.rearrange("n (c h) -> (n c) h", h=P), in_=sums_t[rows : 2 * rows, :]
-        )
+        nc.vector.transpose(out=k_turned[:], in_=k_sums[:])
+        nc.vector.transpose(out=kv_turned[:], in_=kv_sums[:])
+        for q in range(P // QUAD):
+            rows = slice(QUAD * q, QUAD * (q + 1))
+            nc.scalar.dma_start(
+                out=out_1.rearrange("n (c q i) -> q (n c) i", c=CHUNKS, i=QUAD)[q],
+                in_=k_turned[rows, :],
+            )
+            nc.sync.dma_start(
+                out=out_0.rearrange("n (c q i) -> q (n c) i", c=CHUNKS, i=QUAD)[q],
+                in_=kv_turned[rows, :],
+            )

@@ -37,6 +37,11 @@ QUAD = 32
 
 PREPS = BATCH * GROUPS
 VECTOR_COPIES = (PREPS - 1,)
+K_LAG = 2
+SUM_LAG = 3
+SORTED = (0,1,2,3)
+R_UNITS = (5, 9, 13)
+A_UNITS = (3, 7)
 BIAS_AFTER_BATCH = 1
 
 FLOPS = 2 * BATCH * SEQ * FEAT * 2 * CHAN
@@ -48,7 +53,8 @@ def tile_linearattention_pa_kernel(
     nc = tc.nc
     with ExitStack() as ctx:
         keep = ctx.enter_context(tc.tile_pool(name="keep", bufs=1))
-        work = ctx.enter_context(tc.tile_pool(name="work", bufs=4))
+        work = ctx.enter_context(tc.tile_pool(name="work", bufs=6))
+        kpool = ctx.enter_context(tc.tile_pool(name="kpool", bufs=6))
         psum = ctx.enter_context(tc.psum_pool(name="psum", bufs=PSUM_BANKS))
         ctx.enter_context(tc.manual_schedule())
 
@@ -64,7 +70,7 @@ def tile_linearattention_pa_kernel(
         wk_plane = keep.tile([P, GROUPS, CHAN], U8, name="wk_plane", align_bytes=64)
         wv_plane = keep.tile([P, GROUPS, CHAN], U8, name="wv_plane", align_bytes=64)
         ident = keep.tile([P, P], F32, name="ident")
-        bias_rows = keep.tile([P, P], BF16, name="bias_rows")
+        bias_rows = keep.tile([2 * CHUNKS, P], BF16, name="bias_rows")
         bias_rows32 = keep.tile([P, P], F32, name="bias_rows32")
         bias_cols = keep.tile([P, 3 * CHUNKS], F32, name="bias_cols")
         kv_sums = keep.tile([P, SUM_COLS], F32, name="kv_sums", align_bytes=64)
@@ -73,9 +79,13 @@ def tile_linearattention_pa_kernel(
         k_turned = keep.tile([P, SUM_COLS], F32, name="k_turned", align_bytes=64)
         warm = keep.tile([P, 2], F32, name="warm")
 
+        nc.scalar.dma_start(out=bias_rows[0:CHUNKS, :], in_=bk.rearrange("(c h) -> c h", h=P))
+        nc.scalar.dma_start(
+            out=bias_rows[CHUNKS : 2 * CHUNKS, :], in_=bv.rearrange("(c h) -> c h", h=P)
+        )
         nc.vector.memset(warm[:], 0.0)
         nc.scalar.activation(out=warm[:, 1:2], in_=warm[:, 0:1], func=ACT.Exp)
-        nc.vector.memset(bias_rows[:], 0.0)
+        nc.vector.memset(bias_rows32[:], 0.0)
         nc.vector.memset(wk_plane[:].bitcast(I32), 0)
         nc.vector.memset(wv_plane[:].bitcast(I32), 0)
         make_identity(nc, ident[:])
@@ -99,10 +109,6 @@ def tile_linearattention_pa_kernel(
                 in_=words.rearrange("g p b -> p g b")[:, :, b].bitcast(I32),
             )
 
-        nc.scalar.dma_start(out=bias_rows[0:CHUNKS, :], in_=bk.rearrange("(c h) -> c h", h=P))
-        nc.scalar.dma_start(
-            out=bias_rows[CHUNKS : 2 * CHUNKS, :], in_=bv.rearrange("(c h) -> c h", h=P)
-        )
         load_batch(0)
         load_batch(1)
         load_batch(2)
@@ -117,7 +123,7 @@ def tile_linearattention_pa_kernel(
         bias_banks = []
 
         def turn_biases():
-            nc.vector.tensor_copy(out=bias_rows32[:], in_=bias_rows[:])
+            nc.vector.tensor_copy(out=bias_rows32[0 : 2 * CHUNKS, :], in_=bias_rows[:])
             bias_ps = psum.tile([P, N_TOK], F32, tag="bank")
             nc.tensor.transpose(bias_ps[:, 0:P], bias_rows32[:], ident[:])
             bias_banks.append(bias_ps)
@@ -146,11 +152,14 @@ def tile_linearattention_pa_kernel(
                 bank = psum.tile([P, N_TOK], F32, tag="bank")
                 pieces.append(bank[:].rearrange("p (j u t) -> p j u t", j=TILES_PER_BATCH, u=2))
             for j in range(TILES_PER_BATCH):
+                x_words = x_sb[:, n, j, :].bitcast(F32)
                 for g in range(GROUPS):
                     for u in range(2):
-                        nc.tensor.transpose(
-                            pieces[g][:, j, u, :], x_sorted[:, n, j, g, u, :], ident[:]
-                        )
+                        if n in SORTED:
+                            src = x_sorted[:, n, j, g, u, :]
+                        else:
+                            src = x_words[:, 256 * g + u : 256 * (g + 1) : 2]
+                        nc.tensor.transpose(pieces[g][:, j, u, :], src, ident[:])
             for g in range(GROUPS):
                 dst = x_grouped32[:, n, g, :, :].rearrange(
                     "p (j t) u -> p j t u", j=TILES_PER_BATCH
@@ -188,6 +197,7 @@ def tile_linearattention_pa_kernel(
 
         banks = {}
         tiles = {}
+        relus = {}
 
         def start_unit(i):
             half = i // CHUNKS
@@ -198,6 +208,12 @@ def tile_linearattention_pa_kernel(
             nc.scalar.activation(
                 out=expv[:], in_=keyp[:], func=ACT.Exp, bias=bias_cols[:, c : c + 1], scale=1.0
             )
+            if i in R_UNITS:
+                reluv = work.tile([P, N_TOK], F32, tag="reluv")
+                nc.scalar.activation(
+                    out=reluv[:], in_=keyp[:], func=ACT.Relu, bias=bias_cols[:, c : c + 1], scale=1.0
+                )
+                relus[i] = reluv
             capped = work.tile([P, N_TOK], F32, tag="capped")
             if i == 0:
                 nc.vector.tensor_scalar_min(out=capped[:], in0=expv[:], scalar1=1.0)
@@ -207,21 +223,33 @@ def tile_linearattention_pa_kernel(
                 )
             banks[i] = keyp
             tiles[i] = capped
+            if i in R_UNITS:
+                kmat = kpool.tile([P, N_TOK], F32, tag="kmat")
+                nc.gpsimd.tensor_tensor(out=kmat[:], in0=reluv[:], in1=capped[:], op=ALU.add)
+                relus[i] = kmat
 
         def make_k(i):
             half = i // CHUNKS
             c = i % CHUNKS
             value = psum.tile([P, N_TOK], F32, tag="bank")
             product(value, wv_sb, wv_plane, half, c)
-            kmat = work.tile([P, N_TOK], F32, tag="kmat")
-            nc.vector.scalar_tensor_tensor(
-                out=kmat[:],
-                in0=banks[i][:],
-                scalar=bias_cols[:, 2 * CHUNKS + c : 2 * CHUNKS + c + 1],
-                in1=tiles[i][:],
-                op0=ALU.add,
-                op1=ALU.max,
-            )
+            if i in R_UNITS:
+                kmat = relus[i]
+            else:
+                kmat = kpool.tile([P, N_TOK], F32, tag="kmat")
+                cuts = BATCH_PER_HALF if i in A_UNITS else 1
+                for b in range(cuts):
+                    s = slice(b * N_TOK // cuts, (b + 1) * N_TOK // cuts)
+                    col = CHUNKS * (BATCH_PER_HALF * half + b) + c
+                    nc.vector.scalar_tensor_tensor(
+                        out=kmat[:, s],
+                        in0=banks[i][:, s],
+                        scalar=bias_cols[:, 2 * CHUNKS + c : 2 * CHUNKS + c + 1],
+                        in1=tiles[i][:, s],
+                        op0=ALU.add,
+                        op1=ALU.max,
+                        accum_out=k_sums[:, col : col + 1] if i in A_UNITS else None,
+                    )
             banks[i] = value
             tiles[i] = kmat
 
@@ -235,12 +263,13 @@ def tile_linearattention_pa_kernel(
             for b in range(BATCH_PER_HALF):
                 s = slice(b * SEQ, (b + 1) * SEQ)
                 col = CHUNKS * (BATCH_PER_HALF * half + b) + c
-                nc.scalar.activation(
-                    out=copy_of_k[:, s],
-                    in_=kmat[:, s],
-                    func=ACT.Copy,
-                    accum_out=k_sums[:, col : col + 1],
-                )
+                if i not in A_UNITS:
+                    nc.scalar.activation(
+                        out=copy_of_k[:, s],
+                        in_=kmat[:, s],
+                        func=ACT.Copy,
+                        accum_out=k_sums[:, col : col + 1],
+                    )
                 nc.vector.scalar_tensor_tensor(
                     out=prod[:, s],
                     in0=value[:, s],
@@ -251,9 +280,10 @@ def tile_linearattention_pa_kernel(
                     accum_out=kv_sums[:, col : col + 1],
                 )
 
-        sort_words(0)
+        if 0 in SORTED:
+            sort_words(0)
         for n in range(BATCH):
-            if n + 1 < BATCH:
+            if n + 1 in SORTED:
                 sort_words(n + 1)
             turn_batch(n)
             if n > 0:
@@ -265,13 +295,13 @@ def tile_linearattention_pa_kernel(
                 keep_biases()
         for g in range(GROUPS):
             quantise_piece(GROUPS * (BATCH - 1) + g)
-        for step in range(UNITS + 2):
+        for step in range(UNITS + SUM_LAG):
             if step < UNITS:
                 start_unit(step)
-            if 1 <= step <= UNITS:
-                make_k(step - 1)
-            if step >= 2:
-                sum_unit(step - 2)
+            if 0 <= step - K_LAG < UNITS:
+                make_k(step - K_LAG)
+            if step >= SUM_LAG:
+                sum_unit(step - SUM_LAG)
 
         nc.vector.transpose(out=k_turned[:], in_=k_sums[:])
         nc.vector.transpose(out=kv_turned[:], in_=kv_sums[:])

@@ -25,24 +25,19 @@ N_TOK = 512
 HALVES = BATCH * SEQ // N_TOK
 BATCH_PER_HALF = N_TOK // SEQ
 TILES_PER_BATCH = SEQ // P
-TOKEN_TILES = BATCH * SEQ // P
 PSUM_BANKS = 8
 UNITS = HALVES * CHUNKS
 W_PARTS = 2
 PART_BYTES = 2 * CHAN // W_PARTS
 CHUNKS_PER_PART = CHUNKS // W_PARTS
-
 SUM_COLS = BATCH * CHUNKS
 QUAD = 32
 
-PREPS = BATCH * GROUPS
-VECTOR_COPIES = (PREPS - 1,)
+RELU_EVERY = 4
+VECTOR_SUMS = (RELU_EVERY - 1, 2 * RELU_EVERY - 1)
 K_LAG = 2
 SUM_LAG = 3
-SORTED = (0,1,2,3)
-R_UNITS = (5, 9, 13)
-A_UNITS = (3, 7)
-BIAS_AFTER_BATCH = 1
+WORK_BUFS = 6
 
 FLOPS = 2 * BATCH * SEQ * FEAT * 2 * CHAN
 
@@ -53,8 +48,7 @@ def tile_linearattention_pa_kernel(
     nc = tc.nc
     with ExitStack() as ctx:
         keep = ctx.enter_context(tc.tile_pool(name="keep", bufs=1))
-        work = ctx.enter_context(tc.tile_pool(name="work", bufs=6))
-        kpool = ctx.enter_context(tc.tile_pool(name="kpool", bufs=6))
+        work = ctx.enter_context(tc.tile_pool(name="work", bufs=WORK_BUFS))
         psum = ctx.enter_context(tc.psum_pool(name="psum", bufs=PSUM_BANKS))
         ctx.enter_context(tc.manual_schedule())
 
@@ -109,10 +103,8 @@ def tile_linearattention_pa_kernel(
                 in_=words.rearrange("g p b -> p g b")[:, :, b].bitcast(I32),
             )
 
-        load_batch(0)
-        load_batch(1)
-        load_batch(2)
-        load_batch(3)
+        for n in range(BATCH):
+            load_batch(n)
         load_scales(wk_plane, Wk_scales)
         load_words(wk_sb, Wk_words, 0)
         load_scales(wv_plane, Wv_scales)
@@ -122,8 +114,10 @@ def tile_linearattention_pa_kernel(
 
         bias_banks = []
 
-        def turn_biases():
+        def cast_biases():
             nc.vector.tensor_copy(out=bias_rows32[0 : 2 * CHUNKS, :], in_=bias_rows[:])
+
+        def turn_biases():
             bias_ps = psum.tile([P, N_TOK], F32, tag="bank")
             nc.tensor.transpose(bias_ps[:, 0:P], bias_rows32[:], ident[:])
             bias_banks.append(bias_ps)
@@ -137,14 +131,11 @@ def tile_linearattention_pa_kernel(
 
         x_grouped32 = x_grouped[:].bitcast(F32)
 
-        def sort_words(n):
-            for j in range(TILES_PER_BATCH):
-                nc.vector.tensor_copy(
-                    out=x_sorted[:, n, j, :, :, :],
-                    in_=x_sb[:, n, j, :]
-                    .bitcast(F32)
-                    .rearrange("p (g i u) -> p g u i", g=GROUPS, u=2),
-                )
+        def sort_tile(n, j):
+            nc.vector.tensor_copy(
+                out=x_sorted[:, n, j, :, :, :],
+                in_=x_sb[:, n, j, :].bitcast(F32).rearrange("p (g i u) -> p g u i", g=GROUPS, u=2),
+            )
 
         def turn_batch(n):
             pieces = []
@@ -152,27 +143,22 @@ def tile_linearattention_pa_kernel(
                 bank = psum.tile([P, N_TOK], F32, tag="bank")
                 pieces.append(bank[:].rearrange("p (j u t) -> p j u t", j=TILES_PER_BATCH, u=2))
             for j in range(TILES_PER_BATCH):
-                x_words = x_sb[:, n, j, :].bitcast(F32)
                 for g in range(GROUPS):
                     for u in range(2):
-                        if n in SORTED:
-                            src = x_sorted[:, n, j, g, u, :]
-                        else:
-                            src = x_words[:, 256 * g + u : 256 * (g + 1) : 2]
-                        nc.tensor.transpose(pieces[g][:, j, u, :], src, ident[:])
+                        nc.tensor.transpose(
+                            pieces[g][:, j, u, :], x_sorted[:, n, j, g, u, :], ident[:]
+                        )
             for g in range(GROUPS):
                 dst = x_grouped32[:, n, g, :, :].rearrange(
                     "p (j t) u -> p j t u", j=TILES_PER_BATCH
                 )
                 src = pieces[g].rearrange("p j u t -> p j t u")
-                if GROUPS * n + g in VECTOR_COPIES:
+                if n == BATCH - 1 and g == GROUPS - 1:
                     nc.vector.tensor_copy(out=dst, in_=src)
                 else:
                     nc.scalar.copy(out=dst, in_=src)
 
-        def quantise_piece(i):
-            n = i // GROUPS
-            g = i % GROUPS
+        def quantise_piece(n, g):
             cols = slice(n * SEQ, (n + 1) * SEQ)
             nc.vector.quantize_mx(
                 out=x_codes[:, g, cols].bitcast(FP8X4),
@@ -195,9 +181,13 @@ def tile_linearattention_pa_kernel(
                     stop=(g == GROUPS - 1),
                 )
 
-        banks = {}
-        tiles = {}
-        relus = {}
+        keys = {}
+        capped_exps = {}
+        values = {}
+        k_tiles = {}
+
+        def is_relu_unit(i):
+            return i == UNITS - 1 or (i > 0 and i % RELU_EVERY == 0)
 
         def start_unit(i):
             half = i // CHUNKS
@@ -205,15 +195,8 @@ def tile_linearattention_pa_kernel(
             keyp = psum.tile([P, N_TOK], F32, tag="bank")
             product(keyp, wk_sb, wk_plane, half, c)
             expv = work.tile([P, N_TOK], F32, tag="expv")
-            nc.scalar.activation(
-                out=expv[:], in_=keyp[:], func=ACT.Exp, bias=bias_cols[:, c : c + 1], scale=1.0
-            )
-            if i in R_UNITS:
-                reluv = work.tile([P, N_TOK], F32, tag="reluv")
-                nc.scalar.activation(
-                    out=reluv[:], in_=keyp[:], func=ACT.Relu, bias=bias_cols[:, c : c + 1], scale=1.0
-                )
-                relus[i] = reluv
+            bk_col = bias_cols[:, c : c + 1]
+            nc.scalar.activation(out=expv[:], in_=keyp[:], func=ACT.Exp, bias=bk_col, scale=1.0)
             capped = work.tile([P, N_TOK], F32, tag="capped")
             if i == 0:
                 nc.vector.tensor_scalar_min(out=capped[:], in0=expv[:], scalar1=1.0)
@@ -221,80 +204,86 @@ def tile_linearattention_pa_kernel(
                 nc.gpsimd.tensor_scalar(
                     out=capped[:], in0=expv[:], scalar1=1.0, scalar2=0.0, op0=ALU.min, op1=ALU.max
                 )
-            banks[i] = keyp
-            tiles[i] = capped
-            if i in R_UNITS:
-                kmat = kpool.tile([P, N_TOK], F32, tag="kmat")
+            if is_relu_unit(i):
+                reluv = work.tile([P, N_TOK], F32, tag="reluv")
+                nc.scalar.activation(
+                    out=reluv[:], in_=keyp[:], func=ACT.Relu, bias=bk_col, scale=1.0
+                )
+                kmat = work.tile([P, N_TOK], F32, tag="kmat")
                 nc.gpsimd.tensor_tensor(out=kmat[:], in0=reluv[:], in1=capped[:], op=ALU.add)
-                relus[i] = kmat
+                k_tiles[i] = kmat
+            else:
+                keys[i] = keyp
+                capped_exps[i] = capped
+
+        def sum_column(sums, half, b, c):
+            col = CHUNKS * (BATCH_PER_HALF * half + b) + c
+            return sums[:, col : col + 1]
 
         def make_k(i):
             half = i // CHUNKS
             c = i % CHUNKS
             value = psum.tile([P, N_TOK], F32, tag="bank")
             product(value, wv_sb, wv_plane, half, c)
-            if i in R_UNITS:
-                kmat = relus[i]
-            else:
-                kmat = kpool.tile([P, N_TOK], F32, tag="kmat")
-                cuts = BATCH_PER_HALF if i in A_UNITS else 1
-                for b in range(cuts):
-                    s = slice(b * N_TOK // cuts, (b + 1) * N_TOK // cuts)
-                    col = CHUNKS * (BATCH_PER_HALF * half + b) + c
-                    nc.vector.scalar_tensor_tensor(
-                        out=kmat[:, s],
-                        in0=banks[i][:, s],
-                        scalar=bias_cols[:, 2 * CHUNKS + c : 2 * CHUNKS + c + 1],
-                        in1=tiles[i][:, s],
-                        op0=ALU.add,
-                        op1=ALU.max,
-                        accum_out=k_sums[:, col : col + 1] if i in A_UNITS else None,
-                    )
-            banks[i] = value
-            tiles[i] = kmat
+            values[i] = value
+            if is_relu_unit(i):
+                return
+            kmat = work.tile([P, N_TOK], F32, tag="kmat")
+            cuts = BATCH_PER_HALF if i in VECTOR_SUMS else 1
+            for b in range(cuts):
+                s = slice(b * N_TOK // cuts, (b + 1) * N_TOK // cuts)
+                nc.vector.scalar_tensor_tensor(
+                    out=kmat[:, s],
+                    in0=keys[i][:, s],
+                    scalar=bias_cols[:, 2 * CHUNKS + c : 2 * CHUNKS + c + 1],
+                    in1=capped_exps[i][:, s],
+                    op0=ALU.add,
+                    op1=ALU.max,
+                    accum_out=sum_column(k_sums, half, b, c) if i in VECTOR_SUMS else None,
+                )
+            k_tiles[i] = kmat
 
         def sum_unit(i):
             half = i // CHUNKS
             c = i % CHUNKS
-            kmat = tiles[i]
-            value = banks[i]
+            kmat = k_tiles[i]
             copy_of_k = work.tile([P, N_TOK], F32, tag="copy_of_k")
             prod = work.tile([P, N_TOK], F32, tag="prod")
             for b in range(BATCH_PER_HALF):
                 s = slice(b * SEQ, (b + 1) * SEQ)
-                col = CHUNKS * (BATCH_PER_HALF * half + b) + c
-                if i not in A_UNITS:
+                if i not in VECTOR_SUMS:
                     nc.scalar.activation(
                         out=copy_of_k[:, s],
                         in_=kmat[:, s],
                         func=ACT.Copy,
-                        accum_out=k_sums[:, col : col + 1],
+                        accum_out=sum_column(k_sums, half, b, c),
                     )
                 nc.vector.scalar_tensor_tensor(
                     out=prod[:, s],
-                    in0=value[:, s],
+                    in0=values[i][:, s],
                     scalar=bias_cols[:, CHUNKS + c : CHUNKS + c + 1],
                     in1=kmat[:, s],
                     op0=ALU.add,
                     op1=ALU.mult,
-                    accum_out=kv_sums[:, col : col + 1],
+                    accum_out=sum_column(kv_sums, half, b, c),
                 )
 
-        if 0 in SORTED:
-            sort_words(0)
+        for j in range(TILES_PER_BATCH):
+            sort_tile(0, j)
+        cast_biases()
         for n in range(BATCH):
-            if n + 1 in SORTED:
-                sort_words(n + 1)
+            for j in range(TILES_PER_BATCH):
+                if n > 0:
+                    quantise_piece(n - 1, j)
+                if n + 1 < BATCH:
+                    sort_tile(n + 1, j)
             turn_batch(n)
-            if n > 0:
-                for g in range(GROUPS):
-                    quantise_piece(GROUPS * (n - 1) + g)
-            if n == BIAS_AFTER_BATCH:
+            if n == 0:
                 turn_biases()
-            if n == BIAS_AFTER_BATCH + 1:
+            if n == 1:
                 keep_biases()
         for g in range(GROUPS):
-            quantise_piece(GROUPS * (BATCH - 1) + g)
+            quantise_piece(BATCH - 1, g)
         for step in range(UNITS + SUM_LAG):
             if step < UNITS:
                 start_unit(step)

@@ -33,6 +33,7 @@ CHUNKS_PER_PART = CHUNKS // W_PARTS
 SUM_COLS = BATCH * CHUNKS
 QUAD = 32
 
+DUMMIES = (1, 1, 1, 0)
 RELU_EVERY = 4
 VECTOR_SUMS = (RELU_EVERY - 1, 2 * RELU_EVERY - 1)
 K_LAG = 2
@@ -72,6 +73,7 @@ def tile_linearattention_pa_kernel(
         kv_turned = keep.tile([P, SUM_COLS], F32, name="kv_turned", align_bytes=64)
         k_turned = keep.tile([P, SUM_COLS], F32, name="k_turned", align_bytes=64)
         warm = keep.tile([P, 2], F32, name="warm")
+        zeros = keep.tile([P, N_TOK], BF16, name="zeros")
 
         nc.scalar.dma_start(out=bias_rows[0:CHUNKS, :], in_=bk.rearrange("(c h) -> c h", h=P))
         nc.scalar.dma_start(
@@ -80,6 +82,7 @@ def tile_linearattention_pa_kernel(
         nc.vector.memset(warm[:], 0.0)
         nc.scalar.activation(out=warm[:, 1:2], in_=warm[:, 0:1], func=ACT.Exp)
         nc.vector.memset(bias_rows32[:], 0.0)
+        nc.vector.memset(zeros[:], 0.0)
         nc.vector.memset(wk_plane[:].bitcast(I32), 0)
         nc.vector.memset(wv_plane[:].bitcast(I32), 0)
         make_identity(nc, ident[:])
@@ -157,6 +160,11 @@ def tile_linearattention_pa_kernel(
                     nc.vector.tensor_copy(out=dst, in_=src)
                 else:
                     nc.scalar.copy(out=dst, in_=src)
+
+        def keep_warm(n):
+            for d in range(DUMMIES[n]):
+                bank = psum.tile([P, N_TOK], F32, tag="bank")
+                nc.tensor.matmul(out=bank[:], lhsT=zeros[:, 0:P], rhs=zeros[:], start=True, stop=True)
 
         def quantise_piece(n, g):
             cols = slice(n * SEQ, (n + 1) * SEQ)
@@ -280,6 +288,7 @@ def tile_linearattention_pa_kernel(
             turn_batch(n)
             if n == 0:
                 turn_biases()
+            keep_warm(n)
             if n == 1:
                 keep_biases()
         for g in range(GROUPS):

@@ -33,6 +33,7 @@ CHUNKS_PER_PART = CHUNKS // W_PARTS
 SUM_COLS = BATCH * CHUNKS
 QUAD = 32
 
+FIRST_DUMMIES = 5
 DUMMIES = (1, 1, 1, 0)
 RELU_EVERY = 4
 VECTOR_SUMS = (RELU_EVERY - 1, 2 * RELU_EVERY - 1)
@@ -80,9 +81,9 @@ def tile_linearattention_pa_kernel(
             out=bias_rows[CHUNKS : 2 * CHUNKS, :], in_=bv.rearrange("(c h) -> c h", h=P)
         )
         nc.vector.memset(warm[:], 0.0)
+        nc.vector.memset(zeros[:], 0.0)
         nc.scalar.activation(out=warm[:, 1:2], in_=warm[:, 0:1], func=ACT.Exp)
         nc.vector.memset(bias_rows32[:], 0.0)
-        nc.vector.memset(zeros[:], 0.0)
         nc.vector.memset(wk_plane[:].bitcast(I32), 0)
         nc.vector.memset(wv_plane[:].bitcast(I32), 0)
         make_identity(nc, ident[:])
@@ -161,8 +162,8 @@ def tile_linearattention_pa_kernel(
                 else:
                     nc.scalar.copy(out=dst, in_=src)
 
-        def keep_warm(n):
-            for d in range(DUMMIES[n]):
+        def keep_warm(dummies):
+            for d in range(dummies):
                 bank = psum.tile([P, N_TOK], F32, tag="bank")
                 nc.tensor.matmul(out=bank[:], lhsT=zeros[:, 0:P], rhs=zeros[:], start=True, stop=True)
 
@@ -276,6 +277,7 @@ def tile_linearattention_pa_kernel(
                     accum_out=sum_column(kv_sums, half, b, c),
                 )
 
+        keep_warm(FIRST_DUMMIES)
         for j in range(TILES_PER_BATCH):
             sort_tile(0, j)
         cast_biases()
@@ -288,7 +290,7 @@ def tile_linearattention_pa_kernel(
             turn_batch(n)
             if n == 0:
                 turn_biases()
-            keep_warm(n)
+            keep_warm(DUMMIES[n])
             if n == 1:
                 keep_biases()
         for g in range(GROUPS):

@@ -25,6 +25,7 @@ N_TOK = 512
 HALVES = BATCH * SEQ // N_TOK
 BATCH_PER_HALF = N_TOK // SEQ
 TILES_PER_BATCH = SEQ // P
+GROUP_WORDS = K_PASS // 2
 PSUM_BANKS = 8
 UNITS = HALVES * CHUNKS
 W_PARTS = 2
@@ -34,9 +35,11 @@ SUM_COLS = BATCH * CHUNKS
 QUAD = 32
 
 FIRST_DUMMIES = 5
-DUMMIES = (1, 1, 1, 0)
-RELU_EVERY = 4
-VECTOR_SUMS = (RELU_EVERY - 1, 2 * RELU_EVERY - 1)
+DUMMIES = (1, 1, 1)
+RELU_CHUNK = CHUNKS // 2
+VECTOR_SUMS = (1, 5)
+LATE_BATCH = BATCH - 1
+LATE_STEP = 4
 K_LAG = 2
 SUM_LAG = 3
 WORK_BUFS = 6
@@ -107,13 +110,14 @@ def tile_linearattention_pa_kernel(
                 in_=words.rearrange("g p b -> p g b")[:, :, b].bitcast(I32),
             )
 
-        for n in range(BATCH):
+        for n in range(LATE_BATCH):
             load_batch(n)
         load_scales(wk_plane, Wk_scales)
         load_words(wk_sb, Wk_words, 0)
         load_scales(wv_plane, Wv_scales)
         load_words(wv_sb, Wv_words, 0)
         load_words(wk_sb, Wk_words, 1)
+        load_batch(LATE_BATCH)
         load_words(wv_sb, Wv_words, 1)
 
         bias_banks = []
@@ -147,20 +151,20 @@ def tile_linearattention_pa_kernel(
                 bank = psum.tile([P, N_TOK], F32, tag="bank")
                 pieces.append(bank[:].rearrange("p (j u t) -> p j u t", j=TILES_PER_BATCH, u=2))
             for j in range(TILES_PER_BATCH):
+                x_words = x_sb[:, n, j, :].bitcast(F32)
                 for g in range(GROUPS):
                     for u in range(2):
-                        nc.tensor.transpose(
-                            pieces[g][:, j, u, :], x_sorted[:, n, j, g, u, :], ident[:]
-                        )
+                        if n == LATE_BATCH:
+                            words = x_words[:, GROUP_WORDS * g + u : GROUP_WORDS * (g + 1) : 2]
+                        else:
+                            words = x_sorted[:, n, j, g, u, :]
+                        nc.tensor.transpose(pieces[g][:, j, u, :], words, ident[:])
             for g in range(GROUPS):
                 dst = x_grouped32[:, n, g, :, :].rearrange(
                     "p (j t) u -> p j t u", j=TILES_PER_BATCH
                 )
                 src = pieces[g].rearrange("p j u t -> p j t u")
-                if n == BATCH - 1 and g == GROUPS - 1:
-                    nc.vector.tensor_copy(out=dst, in_=src)
-                else:
-                    nc.scalar.copy(out=dst, in_=src)
+                nc.scalar.copy(out=dst, in_=src)
 
         def keep_warm(dummies):
             for d in range(dummies):
@@ -196,7 +200,7 @@ def tile_linearattention_pa_kernel(
         k_tiles = {}
 
         def is_relu_unit(i):
-            return i == UNITS - 1 or (i > 0 and i % RELU_EVERY == 0)
+            return i == UNITS - 1 or i % CHUNKS == RELU_CHUNK
 
         def start_unit(i):
             half = i // CHUNKS
@@ -281,11 +285,11 @@ def tile_linearattention_pa_kernel(
         for j in range(TILES_PER_BATCH):
             sort_tile(0, j)
         cast_biases()
-        for n in range(BATCH):
+        for n in range(LATE_BATCH):
             for j in range(TILES_PER_BATCH):
                 if n > 0:
                     quantise_piece(n - 1, j)
-                if n + 1 < BATCH:
+                if n + 1 < LATE_BATCH:
                     sort_tile(n + 1, j)
             turn_batch(n)
             if n == 0:
@@ -294,10 +298,15 @@ def tile_linearattention_pa_kernel(
             if n == 1:
                 keep_biases()
         for g in range(GROUPS):
-            quantise_piece(BATCH - 1, g)
+            quantise_piece(LATE_BATCH - 1, g)
         for step in range(UNITS + SUM_LAG):
+            if step == LATE_STEP + 2:
+                for g in range(GROUPS):
+                    quantise_piece(LATE_BATCH, g)
             if step < UNITS:
                 start_unit(step)
+            if step == LATE_STEP:
+                turn_batch(LATE_BATCH)
             if 0 <= step - K_LAG < UNITS:
                 make_k(step - K_LAG)
             if step >= SUM_LAG:

@@ -35,11 +35,12 @@ SUM_COLS = BATCH * CHUNKS
 QUAD = 32
 
 FIRST_DUMMIES = 5
-DUMMIES = (1, 1, 1)
+DUMMIES = (2, 1, 1)
 RELU_CHUNK = CHUNKS // 2
 VECTOR_SUMS = (1, 5)
 LATE_BATCH = BATCH - 1
 LATE_STEP = 4
+VECTOR_CAPS = 2
 K_LAG = 2
 SUM_LAG = 3
 WORK_BUFS = 6
@@ -211,7 +212,7 @@ def tile_linearattention_pa_kernel(
             bk_col = bias_cols[:, c : c + 1]
             nc.scalar.activation(out=expv[:], in_=keyp[:], func=ACT.Exp, bias=bk_col, scale=1.0)
             capped = work.tile([P, N_TOK], F32, tag="capped")
-            if i == 0:
+            if i < VECTOR_CAPS:
                 nc.vector.tensor_scalar_min(out=capped[:], in0=expv[:], scalar1=1.0)
             else:
                 nc.gpsimd.tensor_scalar(

from contextlib import ExitStack

import concourse.mybir as mybir
from concourse.masks import make_identity

F32 = mybir.dt.float32
BF16 = mybir.dt.bfloat16
I32 = mybir.dt.int32
U32 = mybir.dt.uint32
U8 = mybir.dt.uint8
FP8X4 = mybir.dt.float8_e4m3fn_x4
FP4X4 = mybir.dt.float4_e2m1fn_x4
ACT = mybir.ActivationFunctionType
ALU = mybir.AluOpType

P = 128
BATCH = 4
SEQ = 256
FEAT = 1024
CHAN = 1024
K_PASS = 512
GROUPS = FEAT // K_PASS
CHUNKS = CHAN // P
N_TOK = 512
HALVES = BATCH * SEQ // N_TOK
BATCH_PER_HALF = N_TOK // SEQ
TILES_PER_BATCH = SEQ // P
GROUP_WORDS = K_PASS // 2
PSUM_BANKS = 8
UNITS = HALVES * CHUNKS
W_PARTS = 2
PART_BYTES = 2 * CHAN // W_PARTS
CHUNKS_PER_PART = CHUNKS // W_PARTS
SUM_COLS = BATCH * CHUNKS
QUAD = 32

FIRST_DUMMIES = 5
DUMMIES = (2, 1, 1)
RELU_CHUNK = CHUNKS // 2
VECTOR_SUMS = (1, 5)
LATE_BATCH = BATCH - 1
LATE_STEP = 4
VECTOR_CAPS = 2
K_LAG = 2
SUM_LAG = 3
WORK_BUFS = 6

FLOPS = 2 * BATCH * SEQ * FEAT * 2 * CHAN


def tile_linearattention_pa_kernel(
    tc, x, Wk_words, Wk_scales, bk, Wv_words, Wv_scales, bv, out_0, out_1
):
    nc = tc.nc
    with ExitStack() as ctx:
        keep = ctx.enter_context(tc.tile_pool(name="keep", bufs=1))
        work = ctx.enter_context(tc.tile_pool(name="work", bufs=WORK_BUFS))
        psum = ctx.enter_context(tc.psum_pool(name="psum", bufs=PSUM_BANKS))
        ctx.enter_context(tc.manual_schedule())

        x_sb = keep.tile([P, BATCH, TILES_PER_BATCH, FEAT], BF16, name="x_sb")
        x_sorted = keep.tile(
            [P, BATCH, TILES_PER_BATCH, GROUPS, 2, P], F32, name="x_sorted", align_bytes=64
        )
        x_grouped = keep.tile([P, BATCH, GROUPS, SEQ, 4], BF16, name="x_grouped", align_bytes=64)
        x_codes = keep.tile([P, GROUPS, BATCH * SEQ], U32, name="x_codes", align_bytes=64)
        x_scales = keep.tile([P, GROUPS, BATCH * SEQ], U8, name="x_scales", align_bytes=64)
        wk_sb = keep.tile([P, W_PARTS, GROUPS, PART_BYTES], U8, name="wk_sb", align_bytes=64)
        wv_sb = keep.tile([P, W_PARTS, GROUPS, PART_BYTES], U8, name="wv_sb", align_bytes=64)
        wk_plane = keep.tile([P, GROUPS, CHAN], U8, name="wk_plane", align_bytes=64)
        wv_plane = keep.tile([P, GROUPS, CHAN], U8, name="wv_plane", align_bytes=64)
        ident = keep.tile([P, P], F32, name="ident")
        bias_rows = keep.tile([2 * CHUNKS, P], BF16, name="bias_rows")
        bias_rows32 = keep.tile([P, P], F32, name="bias_rows32")
        bias_cols = keep.tile([P, 3 * CHUNKS], F32, name="bias_cols")
        kv_sums = keep.tile([P, SUM_COLS], F32, name="kv_sums", align_bytes=64)
        k_sums = keep.tile([P, SUM_COLS], F32, name="k_sums", align_bytes=64)
        kv_turned = keep.tile([P, SUM_COLS], F32, name="kv_turned", align_bytes=64)
        k_turned = keep.tile([P, SUM_COLS], F32, name="k_turned", align_bytes=64)
        warm = keep.tile([P, 2], F32, name="warm")
        zeros = keep.tile([P, N_TOK], BF16, name="zeros")

        nc.scalar.dma_start(out=bias_rows[0:CHUNKS, :], in_=bk.rearrange("(c h) -> c h", h=P))
        nc.scalar.dma_start(
            out=bias_rows[CHUNKS : 2 * CHUNKS, :], in_=bv.rearrange("(c h) -> c h", h=P)
        )
        nc.vector.memset(warm[:], 0.0)
        nc.vector.memset(zeros[:], 0.0)
        nc.scalar.activation(out=warm[:, 1:2], in_=warm[:, 0:1], func=ACT.Exp)
        nc.vector.memset(bias_rows32[:], 0.0)
        nc.vector.memset(wk_plane[:].bitcast(I32), 0)
        nc.vector.memset(wv_plane[:].bitcast(I32), 0)
        make_identity(nc, ident[:])

        def load_batch(n):
            for j in range(TILES_PER_BATCH):
                nc.sync.dma_start(
                    out=x_sb[:, n, j, :],
                    in_=x[n].rearrange("(p j) k -> p j k", j=TILES_PER_BATCH)[:, j, :],
                )

        def load_scales(plane, scales):
            by_r = scales.rearrange("g (q r) n -> r q g n", r=4)
            for r in range(4):
                nc.sync.dma_start(out=plane[r:P:32, :, :].bitcast(I32), in_=by_r[r].bitcast(I32))

        def load_words(words_sb, words, part):
            b = slice(part * PART_BYTES, (part + 1) * PART_BYTES)
            nc.sync.dma_start(
                out=words_sb[:, part, :, :].bitcast(I32),
                in_=words.rearrange("g p b -> p g b")[:, :, b].bitcast(I32),
            )

        for n in range(LATE_BATCH):
            load_batch(n)
        load_scales(wk_plane, Wk_scales)
        load_words(wk_sb, Wk_words, 0)
        load_scales(wv_plane, Wv_scales)
        load_words(wv_sb, Wv_words, 0)
        load_words(wk_sb, Wk_words, 1)
        load_batch(LATE_BATCH)
        load_words(wv_sb, Wv_words, 1)

        bias_banks = []

        def cast_biases():
            nc.vector.tensor_copy(out=bias_rows32[0 : 2 * CHUNKS, :], in_=bias_rows[:])

        def turn_biases():
            bias_ps = psum.tile([P, N_TOK], F32, tag="bank")
            nc.tensor.transpose(bias_ps[:, 0:P], bias_rows32[:], ident[:])
            bias_banks.append(bias_ps)

        def keep_biases():
            bias_ps = bias_banks[0]
            nc.vector.tensor_copy(out=bias_cols[:, 0 : 2 * CHUNKS], in_=bias_ps[:, 0 : 2 * CHUNKS])
            nc.vector.tensor_scalar_add(
                out=bias_cols[:, 2 * CHUNKS : 3 * CHUNKS], in0=bias_cols[:, 0:CHUNKS], scalar1=1.0
            )

        x_grouped32 = x_grouped[:].bitcast(F32)

        def sort_tile(n, j):
            nc.vector.tensor_copy(
                out=x_sorted[:, n, j, :, :, :],
                in_=x_sb[:, n, j, :].bitcast(F32).rearrange("p (g i u) -> p g u i", g=GROUPS, u=2),
            )

        def turn_batch(n):
            pieces = []
            for g in range(GROUPS):
                bank = psum.tile([P, N_TOK], F32, tag="bank")
                pieces.append(bank[:].rearrange("p (j u t) -> p j u t", j=TILES_PER_BATCH, u=2))
            for j in range(TILES_PER_BATCH):
                x_words = x_sb[:, n, j, :].bitcast(F32)
                for g in range(GROUPS):
                    for u in range(2):
                        if n == LATE_BATCH:
                            words = x_words[:, GROUP_WORDS * g + u : GROUP_WORDS * (g + 1) : 2]
                        else:
                            words = x_sorted[:, n, j, g, u, :]
                        nc.tensor.transpose(pieces[g][:, j, u, :], words, ident[:])
            for g in range(GROUPS):
                dst = x_grouped32[:, n, g, :, :].rearrange(
                    "p (j t) u -> p j t u", j=TILES_PER_BATCH
                )
                src = pieces[g].rearrange("p j u t -> p j t u")
                nc.scalar.copy(out=dst, in_=src)

        def keep_warm(dummies):
            for d in range(dummies):
                bank = psum.tile([P, N_TOK], F32, tag="bank")
                nc.tensor.matmul(out=bank[:], lhsT=zeros[:, 0:P], rhs=zeros[:], start=True, stop=True)

        def quantise_piece(n, g):
            cols = slice(n * SEQ, (n + 1) * SEQ)
            nc.vector.quantize_mx(
                out=x_codes[:, g, cols].bitcast(FP8X4),
                scales=x_scales[:, g, cols],
                in_=x_grouped[:, n, g, :, :].rearrange("p t f -> p (t f)"),
            )

        def product(acc, words_sb, plane, half, c):
            cols = slice(half * N_TOK, (half + 1) * N_TOK)
            part = c // CHUNKS_PER_PART
            first = 2 * P * (c % CHUNKS_PER_PART)
            for g in range(GROUPS):
                nc.tensor.matmul_mx(
                    out=acc[:],
                    lhsT=words_sb[:, part, g, first : first + 2 * P].bitcast(FP4X4),
                    lhsT_scale=plane[:, g, P * c : P * (c + 1)],
                    rhs=x_codes[:, g, cols].bitcast(FP8X4),
                    rhs_scale=x_scales[:, g, cols],
                    start=(g == 0),
                    stop=(g == GROUPS - 1),
                )

        keys = {}
        capped_exps = {}
        values = {}
        k_tiles = {}

        def is_relu_unit(i):
            return i == UNITS - 1 or i % CHUNKS == RELU_CHUNK

        def start_unit(i):
            half = i // CHUNKS
            c = i % CHUNKS
            keyp = psum.tile([P, N_TOK], F32, tag="bank")
            product(keyp, wk_sb, wk_plane, half, c)
            expv = work.tile([P, N_TOK], F32, tag="expv")
            bk_col = bias_cols[:, c : c + 1]
            nc.scalar.activation(out=expv[:], in_=keyp[:], func=ACT.Exp, bias=bk_col, scale=1.0)
            capped = work.tile([P, N_TOK], F32, tag="capped")
            if i < VECTOR_CAPS:
                nc.vector.tensor_scalar_min(out=capped[:], in0=expv[:], scalar1=1.0)
            else:
                nc.gpsimd.tensor_scalar(
                    out=capped[:], in0=expv[:], scalar1=1.0, scalar2=0.0, op0=ALU.min, op1=ALU.max
                )
            if is_relu_unit(i):
                reluv = work.tile([P, N_TOK], F32, tag="reluv")
                nc.scalar.activation(
                    out=reluv[:], in_=keyp[:], func=ACT.Relu, bias=bk_col, scale=1.0
                )
                kmat = work.tile([P, N_TOK], F32, tag="kmat")
                nc.gpsimd.tensor_tensor(out=kmat[:], in0=reluv[:], in1=capped[:], op=ALU.add)
                k_tiles[i] = kmat
            else:
                keys[i] = keyp
                capped_exps[i] = capped

        def sum_column(sums, half, b, c):
            col = CHUNKS * (BATCH_PER_HALF * half + b) + c
            return sums[:, col : col + 1]

        def make_k(i):
            half = i // CHUNKS
            c = i % CHUNKS
            value = psum.tile([P, N_TOK], F32, tag="bank")
            product(value, wv_sb, wv_plane, half, c)
            values[i] = value
            if is_relu_unit(i):
                return
            kmat = work.tile([P, N_TOK], F32, tag="kmat")
            cuts = BATCH_PER_HALF if i in VECTOR_SUMS else 1
            for b in range(cuts):
                s = slice(b * N_TOK // cuts, (b + 1) * N_TOK // cuts)
                nc.vector.scalar_tensor_tensor(
                    out=kmat[:, s],
                    in0=keys[i][:, s],
                    scalar=bias_cols[:, 2 * CHUNKS + c : 2 * CHUNKS + c + 1],
                    in1=capped_exps[i][:, s],
                    op0=ALU.add,
                    op1=ALU.max,
                    accum_out=sum_column(k_sums, half, b, c) if i in VECTOR_SUMS else None,
                )
            k_tiles[i] = kmat

        def sum_unit(i):
            half = i // CHUNKS
            c = i % CHUNKS
            kmat = k_tiles[i]
            copy_of_k = work.tile([P, N_TOK], F32, tag="copy_of_k")
            prod = work.tile([P, N_TOK], F32, tag="prod")
            for b in range(BATCH_PER_HALF):
                s = slice(b * SEQ, (b + 1) * SEQ)
                if i not in VECTOR_SUMS:
                    nc.scalar.activation(
                        out=copy_of_k[:, s],
                        in_=kmat[:, s],
                        func=ACT.Copy,
                        accum_out=sum_column(k_sums, half, b, c),
                    )
                nc.vector.scalar_tensor_tensor(
                    out=prod[:, s],
                    in0=values[i][:, s],
                    scalar=bias_cols[:, CHUNKS + c : CHUNKS + c + 1],
                    in1=kmat[:, s],
                    op0=ALU.add,
                    op1=ALU.mult,
                    accum_out=sum_column(kv_sums, half, b, c),
                )

        keep_warm(FIRST_DUMMIES)
        for j in range(TILES_PER_BATCH):
            sort_tile(0, j)
        cast_biases()
        for n in range(LATE_BATCH):
            for j in range(TILES_PER_BATCH):
                if n > 0:
                    quantise_piece(n - 1, j)
                if n + 1 < LATE_BATCH:
                    sort_tile(n + 1, j)
            turn_batch(n)
            if n == 0:
                turn_biases()
            keep_warm(DUMMIES[n])
            if n == 1:
                keep_biases()
        for g in range(GROUPS):
            quantise_piece(LATE_BATCH - 1, g)
        for step in range(UNITS + SUM_LAG):
            if step == LATE_STEP + 2:
                for g in range(GROUPS):
                    quantise_piece(LATE_BATCH, g)
            if step < UNITS:
                start_unit(step)
            if step == LATE_STEP:
                turn_batch(LATE_BATCH)
            if 0 <= step - K_LAG < UNITS:
                make_k(step - K_LAG)
            if step >= SUM_LAG:
                sum_unit(step - SUM_LAG)

        nc.vector.transpose(out=k_turned[:], in_=k_sums[:])
        nc.vector.transpose(out=kv_turned[:], in_=kv_sums[:])
        for q in range(P // QUAD):
            rows = slice(QUAD * q, QUAD * (q + 1))
            nc.scalar.dma_start(
                out=out_1.rearrange("n (c q i) -> q (n c) i", c=CHUNKS, i=QUAD)[q],
                in_=k_turned[rows, :],
            )
            nc.sync.dma_start(
                out=out_0.rearrange("n (c q i) -> q (n c) i", c=CHUNKS, i=QUAD)[q],
                in_=kv_turned[rows, :],
            )
